import numpy as np
import ml_dtypes

BF16 = ml_dtypes.bfloat16


def bf(x):
    return np.asarray(x, np.float32).astype(BF16)


def f32(x):
    return np.asarray(x, np.float32)


def f64(x):
    return np.asarray(x).astype(np.float64)


def striped(idx):
    return np.tile(idx.reshape(-1, 16).T, (8, 1))


D, S, M, N = 128, 2048, 256, 2048
LAM = 0.625


def setup_inputs():
    return {"table": bf(np.maximum(np.random.standard_normal((D, S)), 0.0)), "w": bf(np.random.standard_normal((D, M)) / np.sqrt(D)), "b": f32(0.1 * np.random.standard_normal((M, 1))), "offs": striped(np.random.permutation(S)[:N])}


def reference(table, w, b, offs):
    idx = offs[:16].T.reshape(-1)
    t = f64(table)
    plain = f64(w).T @ t + f64(b)
    shuffled = f64(w).T @ t[:, idx] + f64(b)
    return LAM * plain + (1.0 - LAM) * shuffled

@@ -1,0 +1,51 @@
+import concourse.mybir as mybir
+
+BF16, F32, U16 = mybir.dt.bfloat16, mybir.dt.float32, mybir.dt.uint16
+MULT, ADD = mybir.AluOpType.mult, mybir.AluOpType.add
+IDENTITY = mybir.ActivationFunctionType.Identity
+
+P = 128
+NODES = 2048
+BRANCHES = 2
+PIECE = 512
+PIECES = NODES // PIECE
+OFFS_COLS = PIECE // 16
+LAM = 0.625
+
+FLOPS = 2 * 2 * P * (BRANCHES * P) * NODES
+
+
+def tile_hypermixupmodel_kernel(tc, table, w, b, offs, out):
+    nc = tc.nc
+    blocks = [(j, h) for j in range(PIECES) for h in range(BRANCHES)]
+    with (
+        tc.tile_pool(name="held", bufs=1) as held,
+        tc.tile_pool(name="parts", bufs=len(blocks)) as parts,
+        tc.tile_pool(name="results", bufs=4) as results,
+        tc.psum_pool(name="psum", bufs=8) as psum,
+    ):
+        offsets = held.tile([P, NODES // 16], U16, name="offsets")
+        nc.sync.dma_start(offsets[:], offs)
+        nodes = held.tile([P, NODES], BF16, name="nodes")
+        nc.scalar.dma_start(nodes[:], table)
+        weights = held.tile([P, BRANCHES * P], BF16, name="weights")
+        nc.sync.dma_start(weights[:], w)
+        bias = [held.tile([P, 1], F32, name=f"bias{h}") for h in range(BRANCHES)]
+        for h in range(BRANCHES):
+            nc.gpsimd.dma_start(bias[h][:], b[h * P : (h + 1) * P, :])
+
+
+        plain_part = {}
+        for j, h in blocks:
+            plain = psum.tile([P, PIECE], F32, name="product")
+            nc.tensor.matmul(plain[:], weights[:, h * P : (h + 1) * P], nodes[:, j * PIECE : (j + 1) * PIECE])
+            plain_part[j, h] = parts.tile([P, PIECE], F32, name="plain_part")
+            nc.scalar.activation(plain_part[j, h][:], plain[:], IDENTITY, bias=bias[h][:], scale=LAM)
+
+        for j, h in blocks:
+            shuffled = psum.tile([P, PIECE], F32, name="product")
+            looked_up = nodes[:].indirect(offsets[:, j * OFFS_COLS : (j + 1) * OFFS_COLS])
+            nc.tensor.matmul(shuffled[:], weights[:, h * P : (h + 1) * P], looked_up)
+            mixed = results.tile([P, PIECE], F32, name="mixed")
+            nc.vector.scalar_tensor_tensor(mixed[:], shuffled[:], 1.0 - LAM, plain_part[j, h][:], MULT, ADD)
+            nc.sync.dma_start(out[h * P : (h + 1) * P, j * PIECE : (j + 1) * PIECE], mixed[:])

@@ -21,7 +21,7 @@ def tile_hypermixupmodel_kernel(tc, table, w, b, offs, out):
     with (
         tc.tile_pool(name="held", bufs=1) as held,
         tc.tile_pool(name="parts", bufs=len(blocks)) as parts,
-        tc.tile_pool(name="results", bufs=4) as results,
+        tc.tile_pool(name="results", bufs=len(blocks)) as results,
         tc.psum_pool(name="psum", bufs=8) as psum,
     ):
         offsets = held.tile([P, NODES // 16], U16, name="offsets")

@@ -24,15 +24,17 @@ def tile_hypermixupmodel_kernel(tc, table, w, b, offs, out):
         tc.tile_pool(name="results", bufs=len(blocks)) as results,
         tc.psum_pool(name="psum", bufs=8) as psum,
     ):
-        offsets = held.tile([P, NODES // 16], U16, name="offsets")
-        nc.sync.dma_start(offsets[:], offs)
-        nodes = held.tile([P, NODES], BF16, name="nodes")
-        nc.scalar.dma_start(nodes[:], table)
         weights = held.tile([P, BRANCHES * P], BF16, name="weights")
         nc.sync.dma_start(weights[:], w)
+        nodes = held.tile([P, NODES], BF16, name="nodes")
+        for j in range(PIECES):
+            queue = nc.scalar if j % 2 == 0 else nc.sync
+            queue.dma_start(nodes[:, j * PIECE : (j + 1) * PIECE], table[:, j * PIECE : (j + 1) * PIECE])
         bias = [held.tile([P, 1], F32, name=f"bias{h}") for h in range(BRANCHES)]
         for h in range(BRANCHES):
-            nc.gpsimd.dma_start(bias[h][:], b[h * P : (h + 1) * P, :])
+            nc.sync.dma_start(bias[h][:], b[h * P : (h + 1) * P, :])
+        offsets = held.tile([P, NODES // 16], U16, name="offsets")
+        nc.sync.dma_start(offsets[:], offs)
 
 
         plain_part = {}

@@ -11,6 +11,7 @@ PIECE = 512
 PIECES = NODES // PIECE
 OFFS_COLS = PIECE // 16
 LAM = 0.625
+WARM_UPS = 4
 
 FLOPS = 2 * 2 * P * (BRANCHES * P) * NODES
 
@@ -35,6 +36,12 @@ def tile_hypermixupmodel_kernel(tc, table, w, b, offs, out):
             nc.sync.dma_start(bias[h][:], b[h * P : (h + 1) * P, :])
         offsets = held.tile([P, NODES // 16], U16, name="offsets")
         nc.sync.dma_start(offsets[:], offs)
+
+        zeros = held.tile([P, PIECE], BF16, name="zeros")
+        nc.vector.memset(zeros[:], 0.0)
+        unread = psum.tile([P, PIECE], F32, name="product")
+        for i in range(WARM_UPS):
+            nc.tensor.matmul(unread[:], zeros[:, :P], zeros[:])
 
 
         plain_part = {}

@@ -11,7 +11,6 @@ PIECE = 512
 PIECES = NODES // PIECE
 OFFS_COLS = PIECE // 16
 LAM = 0.625
-WARM_UPS = 4
 
 FLOPS = 2 * 2 * P * (BRANCHES * P) * NODES
 
@@ -37,11 +36,9 @@ def tile_hypermixupmodel_kernel(tc, table, w, b, offs, out):
         offsets = held.tile([P, NODES // 16], U16, name="offsets")
         nc.sync.dma_start(offsets[:], offs)
 
-        zeros = held.tile([P, PIECE], BF16, name="zeros")
-        nc.vector.memset(zeros[:], 0.0)
-        unread = psum.tile([P, PIECE], F32, name="product")
-        for i in range(WARM_UPS):
-            nc.tensor.matmul(unread[:], zeros[:, :P], zeros[:])
+        primer = held.tile([P, 1], F32, name="primer")
+        nc.gpsimd.memset(primer[:], 0.0)
+        nc.scalar.activation(primer[:], primer[:], IDENTITY)
 
 
         plain_part = {}

@@ -11,6 +11,7 @@ PIECE = 512
 PIECES = NODES // PIECE
 OFFS_COLS = PIECE // 16
 LAM = 0.625
+WARM_UPS = 12
 
 FLOPS = 2 * 2 * P * (BRANCHES * P) * NODES
 
@@ -39,6 +40,12 @@ def tile_hypermixupmodel_kernel(tc, table, w, b, offs, out):
         primer = held.tile([P, 1], F32, name="primer")
         nc.gpsimd.memset(primer[:], 0.0)
         nc.scalar.activation(primer[:], primer[:], IDENTITY)
+
+        zeros = held.tile([P, P], BF16, name="zeros")
+        nc.vector.memset(zeros[:], 0.0)
+        unread = psum.tile([P, PIECE], F32, name="product")
+        for i in range(WARM_UPS):
+            nc.tensor.matmul(unread[:, :P], zeros[:], zeros[:])
 
 
         plain_part = {}

@@ -48,17 +48,29 @@ def tile_hypermixupmodel_kernel(tc, table, w, b, offs, out):
             nc.tensor.matmul(unread[:, :P], zeros[:], zeros[:])
 
 
-        plain_part = {}
-        for j, h in blocks:
+        early, late = blocks[:-1], blocks[-1]
+        bracket = {}
+        for j, h in early:
             plain = psum.tile([P, PIECE], F32, name="product")
             nc.tensor.matmul(plain[:], weights[:, h * P : (h + 1) * P], nodes[:, j * PIECE : (j + 1) * PIECE])
-            plain_part[j, h] = parts.tile([P, PIECE], F32, name="plain_part")
-            nc.scalar.activation(plain_part[j, h][:], plain[:], IDENTITY, bias=bias[h][:], scale=LAM)
+            bracket[j, h] = parts.tile([P, PIECE], F32, name="bracket")
+            nc.scalar.activation(bracket[j, h][:], plain[:], IDENTITY, bias=bias[h][:], scale=LAM)
 
-        for j, h in blocks:
+        for j, h in early[:-1] + [late, early[-1]]:
             shuffled = psum.tile([P, PIECE], F32, name="product")
             looked_up = nodes[:].indirect(offsets[:, j * OFFS_COLS : (j + 1) * OFFS_COLS])
             nc.tensor.matmul(shuffled[:], weights[:, h * P : (h + 1) * P], looked_up)
-            mixed = results.tile([P, PIECE], F32, name="mixed")
-            nc.vector.scalar_tensor_tensor(mixed[:], shuffled[:], 1.0 - LAM, plain_part[j, h][:], MULT, ADD)
-            nc.sync.dma_start(out[h * P : (h + 1) * P, j * PIECE : (j + 1) * PIECE], mixed[:])
+            if (j, h) == late:
+                bracket[j, h] = parts.tile([P, PIECE], F32, name="bracket")
+                nc.scalar.activation(bracket[j, h][:], shuffled[:], IDENTITY, bias=bias[h][:], scale=1.0 - LAM)
+            else:
+                mixed = results.tile([P, PIECE], F32, name="mixed")
+                nc.vector.scalar_tensor_tensor(mixed[:], shuffled[:], 1.0 - LAM, bracket[j, h][:], MULT, ADD)
+                nc.sync.dma_start(out[h * P : (h + 1) * P, j * PIECE : (j + 1) * PIECE], mixed[:])
+
+        j, h = late
+        plain = psum.tile([P, PIECE], F32, name="product")
+        nc.tensor.matmul(plain[:], weights[:, h * P : (h + 1) * P], nodes[:, j * PIECE : (j + 1) * PIECE])
+        mixed = results.tile([P, PIECE], F32, name="mixed")
+        nc.vector.scalar_tensor_tensor(mixed[:], plain[:], LAM, bracket[j, h][:], MULT, ADD)
+        nc.sync.dma_start(out[h * P : (h + 1) * P, j * PIECE : (j + 1) * PIECE], mixed[:])

@@ -11,6 +11,7 @@ PIECE = 512
 PIECES = NODES // PIECE
 OFFS_COLS = PIECE // 16
 LAM = 0.625
+NARROW = 44
 WARM_UPS = 12
 
 FLOPS = 2 * 2 * P * (BRANCHES * P) * NODES
@@ -47,30 +48,31 @@ def tile_hypermixupmodel_kernel(tc, table, w, b, offs, out):
         for i in range(WARM_UPS):
             nc.tensor.matmul(unread[:, :P], zeros[:], zeros[:])
 
-
-        early, late = blocks[:-1], blocks[-1]
         bracket = {}
-        for j, h in early:
+
+        def plain_product(j, h, step):
             plain = psum.tile([P, PIECE], F32, name="product")
-            nc.tensor.matmul(plain[:], weights[:, h * P : (h + 1) * P], nodes[:, j * PIECE : (j + 1) * PIECE])
+            for c in range(0, PIECE, step):
+                cols = slice(c, min(c + step, PIECE))
+                moving = nodes[:, j * PIECE + cols.start : j * PIECE + cols.stop]
+                nc.tensor.matmul(plain[:, cols], weights[:, h * P : (h + 1) * P], moving)
             bracket[j, h] = parts.tile([P, PIECE], F32, name="bracket")
             nc.scalar.activation(bracket[j, h][:], plain[:], IDENTITY, bias=bias[h][:], scale=LAM)
 
-        for j, h in early[:-1] + [late, early[-1]]:
+        def shuffled_product(j, h):
             shuffled = psum.tile([P, PIECE], F32, name="product")
             looked_up = nodes[:].indirect(offsets[:, j * OFFS_COLS : (j + 1) * OFFS_COLS])
             nc.tensor.matmul(shuffled[:], weights[:, h * P : (h + 1) * P], looked_up)
-            if (j, h) == late:
-                bracket[j, h] = parts.tile([P, PIECE], F32, name="bracket")
-                nc.scalar.activation(bracket[j, h][:], shuffled[:], IDENTITY, bias=bias[h][:], scale=1.0 - LAM)
-            else:
-                mixed = results.tile([P, PIECE], F32, name="mixed")
-                nc.vector.scalar_tensor_tensor(mixed[:], shuffled[:], 1.0 - LAM, bracket[j, h][:], MULT, ADD)
-                nc.sync.dma_start(out[h * P : (h + 1) * P, j * PIECE : (j + 1) * PIECE], mixed[:])
+            mixed = results.tile([P, PIECE], F32, name="mixed")
+            nc.vector.scalar_tensor_tensor(mixed[:], shuffled[:], 1.0 - LAM, bracket[j, h][:], MULT, ADD)
+            nc.sync.dma_start(out[h * P : (h + 1) * P, j * PIECE : (j + 1) * PIECE], mixed[:])
 
-        j, h = late
-        plain = psum.tile([P, PIECE], F32, name="product")
-        nc.tensor.matmul(plain[:], weights[:, h * P : (h + 1) * P], nodes[:, j * PIECE : (j + 1) * PIECE])
-        mixed = results.tile([P, PIECE], F32, name="mixed")
-        nc.vector.scalar_tensor_tensor(mixed[:], plain[:], LAM, bracket[j, h][:], MULT, ADD)
-        nc.sync.dma_start(out[h * P : (h + 1) * P, j * PIECE : (j + 1) * PIECE], mixed[:])
+        first, last = blocks[:-BRANCHES], blocks[-BRANCHES:]
+        for j, h in first:
+            plain_product(j, h, PIECE)
+        for j, h in first:
+            shuffled_product(j, h)
+        for j, h in last:
+            plain_product(j, h, NARROW)
+        for j, h in last:
+            shuffled_product(j, h)

@@ -57,7 +57,10 @@ def tile_hypermixupmodel_kernel(tc, table, w, b, offs, out):
                 moving = nodes[:, j * PIECE + cols.start : j * PIECE + cols.stop]
                 nc.tensor.matmul(plain[:, cols], weights[:, h * P : (h + 1) * P], moving)
             bracket[j, h] = parts.tile([P, PIECE], F32, name="bracket")
-            nc.scalar.activation(bracket[j, h][:], plain[:], IDENTITY, bias=bias[h][:], scale=LAM)
+            if (j, h) == (0, 1):
+                nc.vector.tensor_scalar(bracket[j, h][:], plain[:], LAM, bias[h][:], MULT, ADD)
+            else:
+                nc.scalar.activation(bracket[j, h][:], plain[:], IDENTITY, bias=bias[h][:], scale=LAM)
 
         def shuffled_product(j, h):
             shuffled = psum.tile([P, PIECE], F32, name="product")

@@ -11,6 +11,7 @@ PIECE = 512
 PIECES = NODES // PIECE
 OFFS_COLS = PIECE // 16
 LAM = 0.625
+AXI = 256
 NARROW = 44
 WARM_UPS = 12
 
@@ -26,16 +27,16 @@ def tile_hypermixupmodel_kernel(tc, table, w, b, offs, out):
         tc.tile_pool(name="results", bufs=len(blocks)) as results,
         tc.psum_pool(name="psum", bufs=8) as psum,
     ):
-        weights = held.tile([P, BRANCHES * P], BF16, name="weights")
+        weights = held.tile([P, BRANCHES * P], BF16, name="weights", align_bytes=AXI)
         nc.sync.dma_start(weights[:], w)
-        nodes = held.tile([P, NODES], BF16, name="nodes")
+        nodes = held.tile([P, NODES], BF16, name="nodes", align_bytes=AXI)
         for j in range(PIECES):
             queue = nc.scalar if j % 2 == 0 else nc.sync
             queue.dma_start(nodes[:, j * PIECE : (j + 1) * PIECE], table[:, j * PIECE : (j + 1) * PIECE])
         bias = [held.tile([P, 1], F32, name=f"bias{h}") for h in range(BRANCHES)]
         for h in range(BRANCHES):
             nc.sync.dma_start(bias[h][:], b[h * P : (h + 1) * P, :])
-        offsets = held.tile([P, NODES // 16], U16, name="offsets")
+        offsets = held.tile([P, NODES // 16], U16, name="offsets", align_bytes=AXI)
         nc.sync.dma_start(offsets[:], offs)
 
         primer = held.tile([P, 1], F32, name="primer")
@@ -66,7 +67,7 @@ def tile_hypermixupmodel_kernel(tc, table, w, b, offs, out):
             shuffled = psum.tile([P, PIECE], F32, name="product")
             looked_up = nodes[:].indirect(offsets[:, j * OFFS_COLS : (j + 1) * OFFS_COLS])
             nc.tensor.matmul(shuffled[:], weights[:, h * P : (h + 1) * P], looked_up)
-            mixed = results.tile([P, PIECE], F32, name="mixed")
+            mixed = results.tile([P, PIECE], F32, name="mixed", align_bytes=AXI)
             nc.vector.scalar_tensor_tensor(mixed[:], shuffled[:], 1.0 - LAM, bracket[j, h][:], MULT, ADD)
             nc.sync.dma_start(out[h * P : (h + 1) * P, j * PIECE : (j + 1) * PIECE], mixed[:])
 

@@ -9,7 +9,7 @@ NODES = 2048
 BRANCHES = 2
 PIECE = 512
 PIECES = NODES // PIECE
-OFFS_COLS = PIECE // 16
+HALF = PIECE // 2
 LAM = 0.625
 AXI = 256
 NARROW = 44
@@ -63,20 +63,22 @@ def tile_hypermixupmodel_kernel(tc, table, w, b, offs, out):
             else:
                 nc.scalar.activation(bracket[j, h][:], plain[:], IDENTITY, bias=bias[h][:], scale=LAM)
 
-        def shuffled_product(j, h):
-            shuffled = psum.tile([P, PIECE], F32, name="product")
-            looked_up = nodes[:].indirect(offsets[:, j * OFFS_COLS : (j + 1) * OFFS_COLS])
-            nc.tensor.matmul(shuffled[:], weights[:, h * P : (h + 1) * P], looked_up)
+        def shuffled_product(j, h, step):
             mixed = results.tile([P, PIECE], F32, name="mixed", align_bytes=AXI)
-            nc.vector.scalar_tensor_tensor(mixed[:], shuffled[:], 1.0 - LAM, bracket[j, h][:], MULT, ADD)
+            for c in range(0, PIECE, step):
+                shuffled = psum.tile([P, step], F32, name="product")
+                entries = offsets[:, (j * PIECE + c) // 16 : (j * PIECE + c + step) // 16]
+                nc.tensor.matmul(shuffled[:], weights[:, h * P : (h + 1) * P], nodes[:].indirect(entries))
+                part = bracket[j, h][:, c : c + step]
+                nc.vector.scalar_tensor_tensor(mixed[:, c : c + step], shuffled[:], 1.0 - LAM, part, MULT, ADD)
             nc.sync.dma_start(out[h * P : (h + 1) * P, j * PIECE : (j + 1) * PIECE], mixed[:])
 
         first, last = blocks[:-BRANCHES], blocks[-BRANCHES:]
         for j, h in first:
             plain_product(j, h, PIECE)
         for j, h in first:
-            shuffled_product(j, h)
+            shuffled_product(j, h, PIECE)
         for j, h in last:
             plain_product(j, h, NARROW)
         for j, h in last:
-            shuffled_product(j, h)
+            shuffled_product(j, h, HALF)

import concourse.mybir as mybir

BF16, F32, U16 = mybir.dt.bfloat16, mybir.dt.float32, mybir.dt.uint16
MULT, ADD = mybir.AluOpType.mult, mybir.AluOpType.add
IDENTITY = mybir.ActivationFunctionType.Identity

P = 128
NODES = 2048
BRANCHES = 2
PIECE = 512
PIECES = NODES // PIECE
HALF = PIECE // 2
LAM = 0.625
AXI = 256
NARROW = 44
WARM_UPS = 12

FLOPS = 2 * 2 * P * (BRANCHES * P) * NODES


def tile_hypermixupmodel_kernel(tc, table, w, b, offs, out):
    nc = tc.nc
    blocks = [(j, h) for j in range(PIECES) for h in range(BRANCHES)]
    with (
        tc.tile_pool(name="held", bufs=1) as held,
        tc.tile_pool(name="parts", bufs=len(blocks)) as parts,
        tc.tile_pool(name="results", bufs=len(blocks)) as results,
        tc.psum_pool(name="psum", bufs=8) as psum,
    ):
        weights = held.tile([P, BRANCHES * P], BF16, name="weights", align_bytes=AXI)
        nc.sync.dma_start(weights[:], w)
        nodes = held.tile([P, NODES], BF16, name="nodes", align_bytes=AXI)
        for j in range(PIECES):
            queue = nc.scalar if j % 2 == 0 else nc.sync
            queue.dma_start(nodes[:, j * PIECE : (j + 1) * PIECE], table[:, j * PIECE : (j + 1) * PIECE])
        bias = [held.tile([P, 1], F32, name=f"bias{h}") for h in range(BRANCHES)]
        for h in range(BRANCHES):
            nc.sync.dma_start(bias[h][:], b[h * P : (h + 1) * P, :])
        offsets = held.tile([P, NODES // 16], U16, name="offsets", align_bytes=AXI)
        nc.sync.dma_start(offsets[:], offs)

        primer = held.tile([P, 1], F32, name="primer")
        nc.gpsimd.memset(primer[:], 0.0)
        nc.scalar.activation(primer[:], primer[:], IDENTITY)

        zeros = held.tile([P, P], BF16, name="zeros")
        nc.vector.memset(zeros[:], 0.0)
        unread = psum.tile([P, PIECE], F32, name="product")
        for i in range(WARM_UPS):
            nc.tensor.matmul(unread[:, :P], zeros[:], zeros[:])

        bracket = {}

        def plain_product(j, h, step):
            plain = psum.tile([P, PIECE], F32, name="product")
            for c in range(0, PIECE, step):
                cols = slice(c, min(c + step, PIECE))
                moving = nodes[:, j * PIECE + cols.start : j * PIECE + cols.stop]
                nc.tensor.matmul(plain[:, cols], weights[:, h * P : (h + 1) * P], moving)
            bracket[j, h] = parts.tile([P, PIECE], F32, name="bracket")
            if (j, h) == (0, 1):
                nc.vector.tensor_scalar(bracket[j, h][:], plain[:], LAM, bias[h][:], MULT, ADD)
            else:
                nc.scalar.activation(bracket[j, h][:], plain[:], IDENTITY, bias=bias[h][:], scale=LAM)

        def shuffled_product(j, h, step):
            mixed = results.tile([P, PIECE], F32, name="mixed", align_bytes=AXI)
            for c in range(0, PIECE, step):
                shuffled = psum.tile([P, step], F32, name="product")
                entries = offsets[:, (j * PIECE + c) // 16 : (j * PIECE + c + step) // 16]
                nc.tensor.matmul(shuffled[:], weights[:, h * P : (h + 1) * P], nodes[:].indirect(entries))
                part = bracket[j, h][:, c : c + step]
                nc.vector.scalar_tensor_tensor(mixed[:, c : c + step], shuffled[:], 1.0 - LAM, part, MULT, ADD)
            nc.sync.dma_start(out[h * P : (h + 1) * P, j * PIECE : (j + 1) * PIECE], mixed[:])

        first, last = blocks[:-BRANCHES], blocks[-BRANCHES:]
        for j, h in first:
            plain_product(j, h, PIECE)
        for j, h in first:
            shuffled_product(j, h, PIECE)
        for j, h in last:
            plain_product(j, h, NARROW)
        for j, h in last:
            shuffled_product(j, h, HALF)
